import numpy as np
import ml_dtypes


def mxq(x, axis, fmt="e4m3"):
    dtype, down = {"e4m3": (ml_dtypes.float8_e4m3fn, 7), "e5m2": (ml_dtypes.float8_e5m2, 14)}[fmt]
    v = np.moveaxis(np.asarray(x, np.float32).astype(ml_dtypes.bfloat16).astype(np.float64), axis, -1)
    blocks = v.reshape(v.shape[:-1] + (-1, 32))
    amax = np.abs(blocks).max(-1, keepdims=True)
    byte = np.maximum(np.where(amax > 0, np.frexp(amax)[1] - 1 + 127, 0) - down, 1)
    scale = np.exp2(byte - 127.0)
    codes = (blocks / scale).astype(np.float32).astype(dtype).astype(np.float64)
    return np.moveaxis((codes * scale).reshape(v.shape), -1, axis)


WIDE = False


def mx_kscale(k):
    if not WIDE:
        return np.ones(k)
    levels = np.array([10, -10, 5, -5, 0])
    a = np.random.permutation(np.resize(levels, k // 512 * 4)).reshape(k // 512, 4)
    idx = np.arange(k)
    return np.exp2(a[idx // 512, idx % 128 // 32])


BF16 = ml_dtypes.bfloat16


def bf(x):
    return np.asarray(x, np.float32).astype(BF16)


def f64(x):
    return np.asarray(x).astype(np.float64)


B, N, CIN, COUT, CB = 8, 512, 1024, 512, 1024
BN_EPS = 1e-5


def batchnorm(x, gamma, beta):
    mu = x.mean(axis=(0, 1))
    var = x.var(axis=(0, 1))
    return gamma * (x - mu) * (1.0 / np.sqrt(var + BN_EPS)) + beta


def setup_inputs():
    s, t = mx_kscale(CIN), mx_kscale(CB)
    return {"feat": bf(np.random.standard_normal((B, N, CIN)) * s),
            "ag": bf(0.4 + 0.12 * np.random.standard_normal((B, N, CB))),
            "W_feat": bf(np.random.standard_normal((CIN, COUT)) / np.sqrt(CIN) / s[:, None]),
            "b_feat": bf(0.3 * np.random.standard_normal(COUT)),
            "g1": bf((1.0 + 0.1 * np.random.standard_normal(CB)) * t),
            "be1": bf(0.1 * np.random.standard_normal(CB) * t),
            "W_ag": bf(np.random.standard_normal((CB, COUT)) / np.sqrt(CB) / t[:, None]),
            "b_ag": bf(0.3 * np.random.standard_normal(COUT))}


def reference(feat, ag, W_feat, b_feat, g1, be1, W_ag, b_ag):
    self_feat = (mxq(f64(feat), 2, "e4m3") @ mxq(f64(W_feat), 0, "e4m3")) + f64(b_feat)
    h = np.maximum(batchnorm(f64(ag), f64(g1), f64(be1)), 0.0)
    ag_proj = (mxq(h, 2, "e4m3") @ mxq(f64(W_ag), 0, "e4m3")) + f64(b_ag)
    return self_feat + ag_proj

@@ -1,0 +1,218 @@
+from contextlib import ExitStack
+
+import concourse.mybir as mybir
+from concourse.masks import make_identity
+
+BF16 = mybir.dt.bfloat16
+F32 = mybir.dt.float32
+U32 = mybir.dt.uint32
+U8 = mybir.dt.uint8
+FP8X4 = mybir.dt.float8_e4m3fn_x4
+ALU = mybir.AluOpType
+ACT = mybir.ActivationFunctionType
+
+P = 128
+PACK = 4
+K_PASS = P * PACK
+
+POINTS = 8 * 512
+CHANNELS = 1024
+COUT = 512
+BN_EPS = 1e-5
+
+SUB = 4
+CHUNK = P * SUB
+N_CHUNKS = POINTS // CHUNK
+PASSES = CHANNELS // K_PASS
+CH_TILES = CHANNELS // P
+BN_STATS_DIM = 6
+RUN = 4
+
+FLOPS = 2 * POINTS * (CHANNELS + CHANNELS) * COUT
+
+
+def by_runs_src(rows):
+    return rows.rearrange("p t (c i) -> p c t i", i=RUN)
+
+
+def by_runs_dst(grouped):
+    return grouped.rearrange("p (c i) t -> p c t i", i=RUN)
+
+
+def tile_geoconv_pb_t_kernel(tc, feat, ag, W_feat, b_feat, g1, be1, W_ag, b_ag, out):
+    nc = tc.nc
+    feat_chunks = feat.flatten_outer_dims().rearrange("(c p i) k -> c p i k", p=P, i=SUB)
+    ag_chunks = ag.flatten_outer_dims().rearrange("(c p i) k -> c p i k", p=P, i=SUB)
+    out_chunks = out.flatten_outer_dims().rearrange("(c p i) n -> c p i n", p=P, i=SUB)
+
+    with ExitStack() as ctx:
+        keep = ctx.enter_context(tc.tile_pool(name="keep", bufs=1))
+        psum = ctx.enter_context(tc.psum_pool(name="psum", bufs=4))
+
+        ident_bf16 = keep.tile([P, P], BF16)
+        make_identity(nc, ident_bf16[:])
+        ident_f32 = keep.tile([P, P], F32)
+        make_identity(nc, ident_f32[:])
+
+        eps = keep.tile([P, 1], F32)
+        nc.vector.memset(eps[:], BN_EPS)
+        table_warmer = keep.tile([P, 1], F32)
+        nc.scalar.activation(out=table_warmer[:], in_=eps[:], func=ACT.Sqrt)
+
+        vector_rows = keep.tile([P, P], BF16)
+        nc.vector.memset(vector_rows[:], 0.0)
+        nc.scalar.dma_start(out=vector_rows[0:CH_TILES, :], in_=g1.rearrange("(j p) -> j p", p=P))
+        nc.scalar.dma_start(out=vector_rows[CH_TILES : 2 * CH_TILES, :], in_=be1.rearrange("(j p) -> j p", p=P))
+        bias_rows = keep.tile([P, COUT], BF16)
+        nc.vector.memset(bias_rows[:], 0.0)
+        nc.scalar.dma_start(out=bias_rows[0:1, :], in_=b_feat.rearrange("(o n) -> o n", o=1))
+        nc.scalar.dma_start(out=bias_rows[1:2, :], in_=b_ag.rearrange("(o n) -> o n", o=1))
+        ones = keep.tile([P, P], BF16)
+        nc.vector.memset(ones[:], 1.0)
+        gain_shift = keep.tile([P, 2 * CH_TILES], F32)
+        gain = gain_shift[:, 0:CH_TILES]
+        shift = gain_shift[:, CH_TILES : 2 * CH_TILES]
+        bias = keep.tile([P, COUT], F32)
+
+        ag_t = keep.tile([P, CH_TILES, POINTS], BF16)
+        feat_grouped = keep.tile([P, N_CHUNKS, PASSES, CHUNK * PACK], BF16, align_bytes=64)
+        feat_grouped_words = feat_grouped[:].bitcast(F32)
+        stats = keep.tile([P, CH_TILES, N_CHUNKS, BN_STATS_DIM], F32)
+        w_codes = keep.tile([P, 2, PASSES, COUT], U32, align_bytes=64)
+        w_scales = keep.tile([P, 2, PASSES, COUT], U8, align_bytes=64)
+        mean_var = keep.tile([P, CH_TILES, 2], F32)
+        std = keep.tile([P, CH_TILES], F32)
+        inv_std = keep.tile([P, CH_TILES], F32)
+        bn_scale = keep.tile([P, CH_TILES], F32)
+        scaled_mean = keep.tile([P, CH_TILES], F32)
+        bn_shift = keep.tile([P, CH_TILES], F32)
+
+        with tc.tile_pool(name="natural", bufs=4) as natural, tc.tile_pool(name="w_stage", bufs=1) as w_stage:
+            for c in range(N_CHUNKS):
+                ag_nat = natural.tile([P, SUB, CHANNELS], BF16, tag="natural")
+                nc.sync.dma_start(out=ag_nat[:], in_=ag_chunks[c])
+                columns = slice(c * CHUNK, (c + 1) * CHUNK)
+                for j0 in range(0, CH_TILES, 2):
+                    bank = psum.tile([P, 2, SUB, P], BF16, tag="transposed")
+                    for jj in range(2):
+                        for i in range(SUB):
+                            j = j0 + jj
+                            nc.tensor.transpose(bank[:, jj, i, :], ag_nat[:, i, j * P : (j + 1) * P], ident_bf16[:])
+                    nc.scalar.copy(out=ag_t[:, j0 : j0 + 2, columns], in_=bank[:].rearrange("p j i q -> p j (i q)"))
+                    for j in range(j0, j0 + 2):
+                        nc.vector.bn_stats(out=stats[:, j, c, :], in_=ag_t[:, j, columns])
+
+            vector_cols = psum.tile([P, P], BF16, tag="transposed")
+            nc.tensor.transpose(vector_cols[:], vector_rows[:], ident_bf16[:])
+            nc.vector.tensor_copy(out=gain_shift[:], in_=vector_cols[:, 0 : 2 * CH_TILES])
+            bias_sum = psum.tile([P, COUT], F32, tag="product")
+            nc.tensor.matmul(out=bias_sum[:], lhsT=ones[:], rhs=bias_rows[:], start=True, stop=True)
+            nc.vector.tensor_copy(out=bias[:], in_=bias_sum[:])
+
+            wf_raw = w_stage.tile([P, PASSES * 2, 2 * COUT], BF16)
+            nc.sync.dma_start(out=wf_raw[:], in_=W_feat.rearrange("(a p e) n -> p a (e n)", p=P, e=2))
+            wa_raw = w_stage.tile([P, PASSES * PACK, COUT], BF16)
+            nc.sync.dma_start(out=wa_raw[:], in_=W_ag.rearrange("(a p) n -> p a n", p=P))
+            w_rows = [wf_raw[:].rearrange("p a (e n) -> p (a e) n", e=2), wa_raw[:]]
+            w_grouped = w_stage.tile([P, 2, PASSES, COUT, PACK], BF16, align_bytes=64)
+            for w in range(2):
+                for g in range(PASSES):
+                    nc.gpsimd.tensor_scalar(
+                        out=by_runs_dst(w_grouped[:, w, g, :, :]),
+                        in0=by_runs_src(w_rows[w][:, g * PACK : (g + 1) * PACK, :]),
+                        scalar1=1.0,
+                        scalar2=0.0,
+                        op0=ALU.mult,
+                        op1=ALU.add,
+                    )
+
+            for c in range(N_CHUNKS):
+                feat_nat = natural.tile([P, SUB, CHANNELS], BF16, tag="natural")
+                nc.sync.dma_start(out=feat_nat[:], in_=feat_chunks[c])
+                feat_words = feat_nat[:].bitcast(F32)
+                for g in range(PASSES):
+                    for i0 in range(0, SUB, 2):
+                        bank = psum.tile([P, 2, 2, P], F32, tag="transposed")
+                        for u in range(2):
+                            for ii in range(2):
+                                first = (2 * g + u) * P
+                                nc.tensor.transpose(
+                                    bank[:, u, ii, :], feat_words[:, i0 + ii, first : first + P], ident_f32[:]
+                                )
+                        nc.scalar.copy(
+                            out=feat_grouped_words[:, c, g, i0 * P * 2 : (i0 + 2) * P * 2].rearrange(
+                                "p (q u) -> p q u", u=2
+                            ),
+                            in_=bank[:].rearrange("p u i q -> p (i q) u"),
+                        )
+
+            for w in range(2):
+                nc.vector.quantize_mx(
+                    out=w_codes[:, w, :, :].rearrange("p g n -> p (g n)").bitcast(FP8X4),
+                    scales=w_scales[:, w, :, :].rearrange("p g n -> p (g n)"),
+                    in_=w_grouped[:, w, :, :, :].rearrange("p g n t -> p (g n t)"),
+                )
+
+        for j in range(CH_TILES):
+            nc.vector.bn_aggr(out=mean_var[:, j, :], in_=stats[:, j, :, :].rearrange("p c s -> p (c s)"))
+        mean = mean_var[:, :, 0]
+        var = mean_var[:, :, 1]
+        nc.scalar.activation(out=std[:], in_=var, func=ACT.Sqrt, bias=eps[:], scale=1.0)
+        nc.vector.reciprocal(out=inv_std[:], in_=std[:])
+        nc.vector.tensor_mul(out=bn_scale[:], in0=gain, in1=inv_std[:])
+        nc.vector.tensor_mul(out=scaled_mean[:], in0=mean, in1=bn_scale[:])
+        nc.vector.tensor_sub(out=bn_shift[:], in0=shift, in1=scaled_mean[:])
+
+        with tc.tile_pool(name="stage", bufs=3) as stage:
+            for c in range(N_CHUNKS):
+                columns = slice(c * CHUNK, (c + 1) * CHUNK)
+                feat_codes = stage.tile([P, PASSES, CHUNK], U32, align_bytes=64)
+                feat_scales = stage.tile([P, PASSES, CHUNK], U8, align_bytes=64)
+                nc.vector.quantize_mx(
+                    out=feat_codes[:].rearrange("p g q -> p (g q)").bitcast(FP8X4),
+                    scales=feat_scales[:].rearrange("p g q -> p (g q)"),
+                    in_=feat_grouped[:, c, :, :].rearrange("p g x -> p (g x)"),
+                )
+                h_codes = stage.tile([P, PASSES, CHUNK], U32, align_bytes=64)
+                h_scales = stage.tile([P, PASSES, CHUNK], U8, align_bytes=64)
+                for g in range(PASSES):
+                    for j in range(g * PACK, (g + 1) * PACK):
+                        nc.vector.tensor_scalar(
+                            out=ag_t[:, j, columns],
+                            in0=ag_t[:, j, columns],
+                            scalar1=bn_scale[:, j : j + 1],
+                            scalar2=bn_shift[:, j : j + 1],
+                            op0=ALU.mult,
+                            op1=ALU.add,
+                        )
+                    h_grouped = stage.tile([P, CHUNK, PACK], BF16, align_bytes=64)
+                    nc.scalar.activation(
+                        out=by_runs_dst(h_grouped[:]),
+                        in_=by_runs_src(ag_t[:, g * PACK : (g + 1) * PACK, columns]),
+                        func=ACT.Relu,
+                    )
+                    nc.vector.quantize_mx(
+                        out=h_codes[:, g, :].bitcast(FP8X4),
+                        scales=h_scales[:, g, :],
+                        in_=h_grouped[:].rearrange("p q t -> p (q t)"),
+                    )
+
+                operands = [(feat_codes, feat_scales), (h_codes, h_scales)]
+                result = stage.tile([P, SUB, COUT], F32)
+                for i in range(SUB):
+                    points = slice(i * P, (i + 1) * P)
+                    product = psum.tile([P, COUT], F32, tag="product")
+                    for w in range(2):
+                        codes, scales = operands[w]
+                        for g in range(PASSES):
+                            nc.tensor.matmul_mx(
+                                out=product[:],
+                                lhsT=codes[:, g, points].bitcast(FP8X4),
+                                lhsT_scale=scales[:, g, points],
+                                rhs=w_codes[:, w, g, :].bitcast(FP8X4),
+                                rhs_scale=w_scales[:, w, g, :],
+                                start=(w == 0 and g == 0),
+                                stop=(w == 1 and g == PASSES - 1),
+                            )
+                    nc.vector.tensor_tensor(out=result[:, i, :], in0=product[:], in1=bias[:], op=ALU.add)
+                nc.sync.dma_start(out=out_chunks[c], in_=result[:])

@@ -26,6 +26,8 @@ N_CHUNKS = POINTS // CHUNK
 PASSES = CHANNELS // K_PASS
 CH_TILES = CHANNELS // P
 BN_STATS_DIM = 6
+PSUM_BANKS = 8
+NATURAL_BUFS = 4
 RUN = 4
 
 FLOPS = 2 * POINTS * (CHANNELS + CHANNELS) * COUT
@@ -46,8 +48,9 @@ def tile_geoconv_pb_t_kernel(tc, feat, ag, W_feat, b_feat, g1, be1, W_ag, b_ag, 
     out_chunks = out.flatten_outer_dims().rearrange("(c p i) n -> c p i n", p=P, i=SUB)
 
     with ExitStack() as ctx:
+        ctx.enter_context(tc.manual_schedule())
         keep = ctx.enter_context(tc.tile_pool(name="keep", bufs=1))
-        psum = ctx.enter_context(tc.psum_pool(name="psum", bufs=4))
+        psum = ctx.enter_context(tc.psum_pool(name="psum", bufs=PSUM_BANKS))
 
         ident_bf16 = keep.tile([P, P], BF16)
         make_identity(nc, ident_bf16[:])
@@ -87,27 +90,18 @@ def tile_geoconv_pb_t_kernel(tc, feat, ag, W_feat, b_feat, g1, be1, W_ag, b_ag, 
         scaled_mean = keep.tile([P, CH_TILES], F32)
         bn_shift = keep.tile([P, CH_TILES], F32)
 
-        with tc.tile_pool(name="natural", bufs=4) as natural, tc.tile_pool(name="w_stage", bufs=1) as w_stage:
-            for c in range(N_CHUNKS):
-                ag_nat = natural.tile([P, SUB, CHANNELS], BF16, tag="natural")
-                nc.sync.dma_start(out=ag_nat[:], in_=ag_chunks[c])
-                columns = slice(c * CHUNK, (c + 1) * CHUNK)
-                for j0 in range(0, CH_TILES, 2):
-                    bank = psum.tile([P, 2, SUB, P], BF16, tag="transposed")
-                    for jj in range(2):
-                        for i in range(SUB):
-                            j = j0 + jj
-                            nc.tensor.transpose(bank[:, jj, i, :], ag_nat[:, i, j * P : (j + 1) * P], ident_bf16[:])
-                    nc.scalar.copy(out=ag_t[:, j0 : j0 + 2, columns], in_=bank[:].rearrange("p j i q -> p j (i q)"))
-                    for j in range(j0, j0 + 2):
-                        nc.vector.bn_stats(out=stats[:, j, c, :], in_=ag_t[:, j, columns])
+        with tc.tile_pool(name="w_stage", bufs=1) as w_stage, tc.tile_pool(name="natural", bufs=NATURAL_BUFS) as natural:
+            sources = [ag_chunks[c] for c in range(N_CHUNKS)] + [feat_chunks[c] for c in range(N_CHUNKS)]
+            loaded = []
 
-            vector_cols = psum.tile([P, P], BF16, tag="transposed")
-            nc.tensor.transpose(vector_cols[:], vector_rows[:], ident_bf16[:])
-            nc.vector.tensor_copy(out=gain_shift[:], in_=vector_cols[:, 0 : 2 * CH_TILES])
-            bias_sum = psum.tile([P, COUT], F32, tag="product")
-            nc.tensor.matmul(out=bias_sum[:], lhsT=ones[:], rhs=bias_rows[:], start=True, stop=True)
-            nc.vector.tensor_copy(out=bias[:], in_=bias_sum[:])
+            def load_next_chunk():
+                if len(loaded) < len(sources):
+                    chunk = natural.tile([P, SUB, CHANNELS], BF16, tag="natural", name="chunk")
+                    nc.sync.dma_start(out=chunk[:], in_=sources[len(loaded)])
+                    loaded.append(chunk)
+
+            for k in range(NATURAL_BUFS):
+                load_next_chunk()
 
             wf_raw = w_stage.tile([P, PASSES * 2, 2 * COUT], BF16)
             nc.sync.dma_start(out=wf_raw[:], in_=W_feat.rearrange("(a p e) n -> p a (e n)", p=P, e=2))
@@ -127,12 +121,28 @@ def tile_geoconv_pb_t_kernel(tc, feat, ag, W_feat, b_feat, g1, be1, W_ag, b_ag, 
                     )
 
             for c in range(N_CHUNKS):
-                feat_nat = natural.tile([P, SUB, CHANNELS], BF16, tag="natural")
-                nc.sync.dma_start(out=feat_nat[:], in_=feat_chunks[c])
-                feat_words = feat_nat[:].bitcast(F32)
+                ag_nat = loaded[c]
+                columns = slice(c * CHUNK, (c + 1) * CHUNK)
+                for j in range(CH_TILES):
+                    bank = psum.tile([P, SUB, P], BF16, tag="bank")
+                    for i in range(SUB):
+                        nc.tensor.transpose(bank[:, i, :], ag_nat[:, i, j * P : (j + 1) * P], ident_bf16[:])
+                    nc.scalar.copy(out=ag_t[:, j, columns], in_=bank[:].rearrange("p i q -> p (i q)"))
+                    nc.vector.bn_stats(out=stats[:, j, c, :], in_=ag_t[:, j, columns])
+                load_next_chunk()
+
+            vector_cols = psum.tile([P, P], BF16, tag="bank")
+            nc.tensor.transpose(vector_cols[:], vector_rows[:], ident_bf16[:])
+            nc.scalar.copy(out=gain_shift[:], in_=vector_cols[:, 0 : 2 * CH_TILES])
+            bias_sum = psum.tile([P, COUT], F32, tag="bank")
+            nc.tensor.matmul(out=bias_sum[:], lhsT=ones[:], rhs=bias_rows[:], start=True, stop=True)
+            nc.scalar.copy(out=bias[:], in_=bias_sum[:])
+
+            for c in range(N_CHUNKS):
+                feat_words = loaded[N_CHUNKS + c][:].bitcast(F32)
                 for g in range(PASSES):
                     for i0 in range(0, SUB, 2):
-                        bank = psum.tile([P, 2, 2, P], F32, tag="transposed")
+                        bank = psum.tile([P, 2, 2, P], F32, tag="bank")
                         for u in range(2):
                             for ii in range(2):
                                 first = (2 * g + u) * P
@@ -145,65 +155,81 @@ def tile_geoconv_pb_t_kernel(tc, feat, ag, W_feat, b_feat, g1, be1, W_ag, b_ag, 
                             ),
                             in_=bank[:].rearrange("p u i q -> p (i q) u"),
                         )
+                load_next_chunk()
 
+            for j in range(CH_TILES):
+                nc.vector.bn_aggr(out=mean_var[:, j, :], in_=stats[:, j, :, :].rearrange("p c s -> p (c s)"))
+            mean = mean_var[:, :, 0]
+            var = mean_var[:, :, 1]
+            nc.scalar.activation(out=std[:], in_=var, func=ACT.Sqrt, bias=eps[:], scale=1.0)
             for w in range(2):
                 nc.vector.quantize_mx(
                     out=w_codes[:, w, :, :].rearrange("p g n -> p (g n)").bitcast(FP8X4),
                     scales=w_scales[:, w, :, :].rearrange("p g n -> p (g n)"),
                     in_=w_grouped[:, w, :, :, :].rearrange("p g n t -> p (g n t)"),
                 )
+            nc.vector.reciprocal(out=inv_std[:], in_=std[:])
+            nc.vector.tensor_mul(out=bn_scale[:], in0=gain, in1=inv_std[:])
+            nc.vector.tensor_mul(out=scaled_mean[:], in0=mean, in1=bn_scale[:])
+            nc.vector.tensor_sub(out=bn_shift[:], in0=shift, in1=scaled_mean[:])
 
-        for j in range(CH_TILES):
-            nc.vector.bn_aggr(out=mean_var[:, j, :], in_=stats[:, j, :, :].rearrange("p c s -> p (c s)"))
-        mean = mean_var[:, :, 0]
-        var = mean_var[:, :, 1]
-        nc.scalar.activation(out=std[:], in_=var, func=ACT.Sqrt, bias=eps[:], scale=1.0)
-        nc.vector.reciprocal(out=inv_std[:], in_=std[:])
-        nc.vector.tensor_mul(out=bn_scale[:], in0=gain, in1=inv_std[:])
-        nc.vector.tensor_mul(out=scaled_mean[:], in0=mean, in1=bn_scale[:])
-        nc.vector.tensor_sub(out=bn_shift[:], in0=shift, in1=scaled_mean[:])
+        with tc.tile_pool(name="stage", bufs=2, reuse_waits="tile") as stage, tc.tile_pool(
+            name="codes", bufs=3, reuse_waits="tile"
+        ) as codes_pool:
+            h_grouped = {}
+            operands = {}
+            products = {}
 
-        with tc.tile_pool(name="stage", bufs=3) as stage:
-            for c in range(N_CHUNKS):
+            def batch_norm(c):
                 columns = slice(c * CHUNK, (c + 1) * CHUNK)
-                feat_codes = stage.tile([P, PASSES, CHUNK], U32, align_bytes=64)
-                feat_scales = stage.tile([P, PASSES, CHUNK], U8, align_bytes=64)
+                for j in range(CH_TILES):
+                    nc.vector.tensor_scalar(
+                        out=ag_t[:, j, columns],
+                        in0=ag_t[:, j, columns],
+                        scalar1=bn_scale[:, j : j + 1],
+                        scalar2=bn_shift[:, j : j + 1],
+                        op0=ALU.mult,
+                        op1=ALU.add,
+                    )
+
+            def relu_and_regroup(c):
+                columns = slice(c * CHUNK, (c + 1) * CHUNK)
+                h_grouped[c] = stage.tile([P, PASSES, CHUNK, PACK], BF16, align_bytes=64, name="h_grouped")
+                for g in range(PASSES):
+                    nc.scalar.activation(
+                        out=by_runs_dst(h_grouped[c][:, g, :, :]),
+                        in_=by_runs_src(ag_t[:, g * PACK : (g + 1) * PACK, columns]),
+                        func=ACT.Relu,
+                    )
+
+            def quantise_feat(c):
+                feat_codes = codes_pool.tile([P, PASSES, CHUNK], U32, align_bytes=64)
+                feat_scales = codes_pool.tile([P, PASSES, CHUNK], U8, align_bytes=64)
                 nc.vector.quantize_mx(
                     out=feat_codes[:].rearrange("p g q -> p (g q)").bitcast(FP8X4),
                     scales=feat_scales[:].rearrange("p g q -> p (g q)"),
                     in_=feat_grouped[:, c, :, :].rearrange("p g x -> p (g x)"),
                 )
-                h_codes = stage.tile([P, PASSES, CHUNK], U32, align_bytes=64)
-                h_scales = stage.tile([P, PASSES, CHUNK], U8, align_bytes=64)
+                operands[c] = [(feat_codes, feat_scales)]
+
+            def quantise_h(c):
+                h_codes = codes_pool.tile([P, PASSES, CHUNK], U32, align_bytes=64)
+                h_scales = codes_pool.tile([P, PASSES, CHUNK], U8, align_bytes=64)
                 for g in range(PASSES):
-                    for j in range(g * PACK, (g + 1) * PACK):
-                        nc.vector.tensor_scalar(
-                            out=ag_t[:, j, columns],
-                            in0=ag_t[:, j, columns],
-                            scalar1=bn_scale[:, j : j + 1],
-                            scalar2=bn_shift[:, j : j + 1],
-                            op0=ALU.mult,
-                            op1=ALU.add,
-                        )
-                    h_grouped = stage.tile([P, CHUNK, PACK], BF16, align_bytes=64)
-                    nc.scalar.activation(
-                        out=by_runs_dst(h_grouped[:]),
-                        in_=by_runs_src(ag_t[:, g * PACK : (g + 1) * PACK, columns]),
-                        func=ACT.Relu,
-                    )
                     nc.vector.quantize_mx(
                         out=h_codes[:, g, :].bitcast(FP8X4),
                         scales=h_scales[:, g, :],
-                        in_=h_grouped[:].rearrange("p q t -> p (q t)"),
+                        in_=h_grouped[c][:, g, :, :].rearrange("p q t -> p (q t)"),
                     )
+                operands[c].append((h_codes, h_scales))
 
-                operands = [(feat_codes, feat_scales), (h_codes, h_scales)]
-                result = stage.tile([P, SUB, COUT], F32)
+            def multiply(c):
+                products[c] = []
                 for i in range(SUB):
                     points = slice(i * P, (i + 1) * P)
-                    product = psum.tile([P, COUT], F32, tag="product")
+                    product = psum.tile([P, COUT], F32, tag="bank")
                     for w in range(2):
-                        codes, scales = operands[w]
+                        codes, scales = operands[c][w]
                         for g in range(PASSES):
                             nc.tensor.matmul_mx(
                                 out=product[:],
@@ -214,5 +240,23 @@ def tile_geoconv_pb_t_kernel(tc, feat, ag, W_feat, b_feat, g1, be1, W_ag, b_ag, 
                                 start=(w == 0 and g == 0),
                                 stop=(w == 1 and g == PASSES - 1),
                             )
-                    nc.vector.tensor_tensor(out=result[:, i, :], in0=product[:], in1=bias[:], op=ALU.add)
-                nc.sync.dma_start(out=out_chunks[c], in_=result[:])
+                    products[c].append(product)
+
+            def add_bias_and_store(c):
+                result = stage.tile([P, SUB, COUT], F32)
+                for i in range(SUB):
+                    nc.vector.tensor_tensor(out=result[:, i, :], in0=products[c][i][:], in1=bias[:], op=ALU.add)
+                    if i % 2 == 1:
+                        nc.sync.dma_start(out=out_chunks[c][:, i - 1 : i + 1, :], in_=result[:, i - 1 : i + 1, :])
+
+            for k in range(-2, N_CHUNKS + 1):
+                if k + 2 < N_CHUNKS:
+                    batch_norm(k + 2)
+                if 0 <= k + 1 < N_CHUNKS:
+                    relu_and_regroup(k + 1)
+                    quantise_feat(k + 1)
+                if 0 <= k < N_CHUNKS:
+                    quantise_h(k)
+                    multiply(k)
+                if 0 <= k - 1:
+                    add_bias_and_store(k - 1)

@@ -180,18 +180,6 @@ def tile_geoconv_pb_t_kernel(tc, feat, ag, W_feat, b_feat, g1, be1, W_ag, b_ag, 
             operands = {}
             products = {}
 
-            def batch_norm(c):
-                columns = slice(c * CHUNK, (c + 1) * CHUNK)
-                for j in range(CH_TILES):
-                    nc.vector.tensor_scalar(
-                        out=ag_t[:, j, columns],
-                        in0=ag_t[:, j, columns],
-                        scalar1=bn_scale[:, j : j + 1],
-                        scalar2=bn_shift[:, j : j + 1],
-                        op0=ALU.mult,
-                        op1=ALU.add,
-                    )
-
             def relu_and_regroup(c):
                 columns = slice(c * CHUNK, (c + 1) * CHUNK)
                 h_grouped[c] = stage.tile([P, PASSES, CHUNK, PACK], BF16, align_bytes=64, name="h_grouped")
@@ -215,24 +203,22 @@ def tile_geoconv_pb_t_kernel(tc, feat, ag, W_feat, b_feat, g1, be1, W_ag, b_ag, 
             def quantise_h(c):
                 h_codes = codes_pool.tile([P, PASSES, CHUNK], U32, align_bytes=64)
                 h_scales = codes_pool.tile([P, PASSES, CHUNK], U8, align_bytes=64)
-                for g in range(PASSES):
-                    nc.vector.quantize_mx(
-                        out=h_codes[:, g, :].bitcast(FP8X4),
-                        scales=h_scales[:, g, :],
-                        in_=h_grouped[c][:, g, :, :].rearrange("p q t -> p (q t)"),
-                    )
+                nc.vector.quantize_mx(
+                    out=h_codes[:].rearrange("p g q -> p (g q)").bitcast(FP8X4),
+                    scales=h_scales[:].rearrange("p g q -> p (g q)"),
+                    in_=h_grouped[c][:].rearrange("p g q t -> p (g q t)"),
+                )
                 operands[c].append((h_codes, h_scales))
 
             def multiply(c):
-                products[c] = []
-                for i in range(SUB):
-                    points = slice(i * P, (i + 1) * P)
-                    product = psum.tile([P, COUT], F32, tag="bank")
-                    for w in range(2):
-                        codes, scales = operands[c][w]
-                        for g in range(PASSES):
+                products[c] = [psum.tile([P, COUT], F32, tag="bank", name="product") for i in range(SUB)]
+                for w in range(2):
+                    codes, scales = operands[c][w]
+                    for g in range(PASSES):
+                        for i in range(SUB):
+                            points = slice(i * P, (i + 1) * P)
                             nc.tensor.matmul_mx(
-                                out=product[:],
+                                out=products[c][i][:],
                                 lhsT=codes[:, g, points].bitcast(FP8X4),
                                 lhsT_scale=scales[:, g, points],
                                 rhs=w_codes[:, w, g, :].bitcast(FP8X4),
@@ -240,7 +226,6 @@ def tile_geoconv_pb_t_kernel(tc, feat, ag, W_feat, b_feat, g1, be1, W_ag, b_ag, 
                                 start=(w == 0 and g == 0),
                                 stop=(w == 1 and g == PASSES - 1),
                             )
-                    products[c].append(product)
 
             def add_bias_and_store(c):
                 result = stage.tile([P, SUB, COUT], F32)
@@ -249,10 +234,18 @@ def tile_geoconv_pb_t_kernel(tc, feat, ag, W_feat, b_feat, g1, be1, W_ag, b_ag, 
                     if i % 2 == 1:
                         nc.sync.dma_start(out=out_chunks[c][:, i - 1 : i + 1, :], in_=result[:, i - 1 : i + 1, :])
 
-            for k in range(-2, N_CHUNKS + 1):
-                if k + 2 < N_CHUNKS:
-                    batch_norm(k + 2)
-                if 0 <= k + 1 < N_CHUNKS:
+            for j in range(CH_TILES):
+                nc.vector.tensor_scalar(
+                    out=ag_t[:, j, :],
+                    in0=ag_t[:, j, :],
+                    scalar1=bn_scale[:, j : j + 1],
+                    scalar2=bn_shift[:, j : j + 1],
+                    op0=ALU.mult,
+                    op1=ALU.add,
+                )
+
+            for k in range(-1, N_CHUNKS + 1):
+                if k + 1 < N_CHUNKS:
                     relu_and_regroup(k + 1)
                     quantise_feat(k + 1)
                 if 0 <= k < N_CHUNKS:

@@ -10,6 +10,7 @@ U8 = mybir.dt.uint8
 FP8X4 = mybir.dt.float8_e4m3fn_x4
 ALU = mybir.AluOpType
 ACT = mybir.ActivationFunctionType
+AXIS = mybir.AxisListType
 
 P = 128
 PACK = 4
@@ -27,7 +28,11 @@ PASSES = CHANNELS // K_PASS
 CH_TILES = CHANNELS // P
 BN_STATS_DIM = 6
 PSUM_BANKS = 8
-NATURAL_BUFS = 4
+NATURAL_BUFS = 5
+PE_STAT_TILES = 3
+DVE_STAT_TILES = CH_TILES - PE_STAT_TILES
+FEAT_EARLY = 2
+FEAT_AHEAD = 3
 RUN = 4
 
 FLOPS = 2 * POINTS * (CHANNELS + CHANNELS) * COUT
@@ -50,7 +55,6 @@ def tile_geoconv_pb_t_kernel(tc, feat, ag, W_feat, b_feat, g1, be1, W_ag, b_ag, 
     with ExitStack() as ctx:
         ctx.enter_context(tc.manual_schedule())
         keep = ctx.enter_context(tc.tile_pool(name="keep", bufs=1))
-        psum = ctx.enter_context(tc.psum_pool(name="psum", bufs=PSUM_BANKS))
 
         ident_bf16 = keep.tile([P, P], BF16)
         make_identity(nc, ident_bf16[:])
@@ -62,6 +66,8 @@ def tile_geoconv_pb_t_kernel(tc, feat, ag, W_feat, b_feat, g1, be1, W_ag, b_ag, 
         table_warmer = keep.tile([P, 1], F32)
         nc.scalar.activation(out=table_warmer[:], in_=eps[:], func=ACT.Sqrt)
 
+        ones = keep.tile([P, P], BF16)
+        nc.vector.memset(ones[:], 1.0)
         vector_rows = keep.tile([P, P], BF16)
         nc.vector.memset(vector_rows[:], 0.0)
         nc.scalar.dma_start(out=vector_rows[0:CH_TILES, :], in_=g1.rearrange("(j p) -> j p", p=P))
@@ -70,8 +76,6 @@ def tile_geoconv_pb_t_kernel(tc, feat, ag, W_feat, b_feat, g1, be1, W_ag, b_ag, 
         nc.vector.memset(bias_rows[:], 0.0)
         nc.scalar.dma_start(out=bias_rows[0:1, :], in_=b_feat.rearrange("(o n) -> o n", o=1))
         nc.scalar.dma_start(out=bias_rows[1:2, :], in_=b_ag.rearrange("(o n) -> o n", o=1))
-        ones = keep.tile([P, P], BF16)
-        nc.vector.memset(ones[:], 1.0)
         gain_shift = keep.tile([P, 2 * CH_TILES], F32)
         gain = gain_shift[:, 0:CH_TILES]
         shift = gain_shift[:, CH_TILES : 2 * CH_TILES]
@@ -80,17 +84,30 @@ def tile_geoconv_pb_t_kernel(tc, feat, ag, W_feat, b_feat, g1, be1, W_ag, b_ag, 
         ag_t = keep.tile([P, CH_TILES, POINTS], BF16)
         feat_grouped = keep.tile([P, N_CHUNKS, PASSES, CHUNK * PACK], BF16, align_bytes=64)
         feat_grouped_words = feat_grouped[:].bitcast(F32)
-        stats = keep.tile([P, CH_TILES, N_CHUNKS, BN_STATS_DIM], F32)
         w_codes = keep.tile([P, 2, PASSES, COUT], U32, align_bytes=64)
         w_scales = keep.tile([P, 2, PASSES, COUT], U8, align_bytes=64)
+        stats = keep.tile([P, DVE_STAT_TILES, N_CHUNKS, BN_STATS_DIM], F32)
+        diagonal = keep.tile([P, PE_STAT_TILES, P], F32)
+        sum_of_squares = keep.tile([P, PE_STAT_TILES], F32)
+        sum_of_values = keep.tile([P, PE_STAT_TILES], F32)
+        mean_squared = keep.tile([P, PE_STAT_TILES], F32)
         mean_var = keep.tile([P, CH_TILES, 2], F32)
+        mean = mean_var[:, :, 0]
+        var = mean_var[:, :, 1]
         std = keep.tile([P, CH_TILES], F32)
         inv_std = keep.tile([P, CH_TILES], F32)
         bn_scale = keep.tile([P, CH_TILES], F32)
         scaled_mean = keep.tile([P, CH_TILES], F32)
         bn_shift = keep.tile([P, CH_TILES], F32)
 
-        with tc.tile_pool(name="w_stage", bufs=1) as w_stage, tc.tile_pool(name="natural", bufs=NATURAL_BUFS) as natural:
+        with ExitStack() as part1:
+            w_stage = part1.enter_context(tc.tile_pool(name="w_stage", bufs=1))
+            natural = part1.enter_context(tc.tile_pool(name="natural", bufs=NATURAL_BUFS))
+            sums_psum = part1.enter_context(tc.psum_pool(name="sums_psum", bufs=1))
+            turned = part1.enter_context(tc.psum_pool(name="turned", bufs=PSUM_BANKS - PE_STAT_TILES - 1))
+            squares = [sums_psum.tile([P, P], F32, name="squares%d" % s) for s in range(PE_STAT_TILES)]
+            values = sums_psum.tile([P, PE_STAT_TILES, N_CHUNKS * SUB, 2], F32)
+
             sources = [ag_chunks[c] for c in range(N_CHUNKS)] + [feat_chunks[c] for c in range(N_CHUNKS)]
             loaded = []
 
@@ -124,25 +141,42 @@ def tile_geoconv_pb_t_kernel(tc, feat, ag, W_feat, b_feat, g1, be1, W_ag, b_ag, 
                 ag_nat = loaded[c]
                 columns = slice(c * CHUNK, (c + 1) * CHUNK)
                 for j in range(CH_TILES):
-                    bank = psum.tile([P, SUB, P], BF16, tag="bank")
+                    blocks = [ag_nat[:, i, j * P : (j + 1) * P] for i in range(SUB)]
+                    bank = turned.tile([P, SUB, P], BF16, tag="bank")
                     for i in range(SUB):
-                        nc.tensor.transpose(bank[:, i, :], ag_nat[:, i, j * P : (j + 1) * P], ident_bf16[:])
-                    nc.scalar.copy(out=ag_t[:, j, columns], in_=bank[:].rearrange("p i q -> p (i q)"))
-                    nc.vector.bn_stats(out=stats[:, j, c, :], in_=ag_t[:, j, columns])
+                        nc.tensor.transpose(bank[:, i, :], blocks[i], ident_bf16[:])
+                    nc.scalar.copy(
+                        out=ag_t[:, j, columns].bitcast(F32), in_=bank[:].rearrange("p i q -> p (i q)").bitcast(F32)
+                    )
+                    if j < DVE_STAT_TILES:
+                        nc.vector.bn_stats(out=stats[:, j, c, :], in_=ag_t[:, j, columns])
+                    else:
+                        s = j - DVE_STAT_TILES
+                        for i in range(SUB):
+                            nc.tensor.matmul(
+                                out=squares[s][:],
+                                lhsT=blocks[i],
+                                rhs=blocks[i],
+                                start=(c == 0 and i == 0),
+                                stop=(c == N_CHUNKS - 1 and i == SUB - 1),
+                            )
+                            nc.tensor.matmul(
+                                out=values[:, s, c * SUB + i, :], lhsT=blocks[i], rhs=ones[:, 0:2], start=True, stop=True
+                            )
                 load_next_chunk()
 
-            vector_cols = psum.tile([P, P], BF16, tag="bank")
+            vector_cols = turned.tile([P, P], BF16, tag="bank")
             nc.tensor.transpose(vector_cols[:], vector_rows[:], ident_bf16[:])
             nc.scalar.copy(out=gain_shift[:], in_=vector_cols[:, 0 : 2 * CH_TILES])
-            bias_sum = psum.tile([P, COUT], F32, tag="bank")
+            bias_sum = turned.tile([P, COUT], F32, tag="bank")
             nc.tensor.matmul(out=bias_sum[:], lhsT=ones[:], rhs=bias_rows[:], start=True, stop=True)
             nc.scalar.copy(out=bias[:], in_=bias_sum[:])
 
-            for c in range(N_CHUNKS):
+            def transpose_feat(c):
                 feat_words = loaded[N_CHUNKS + c][:].bitcast(F32)
                 for g in range(PASSES):
                     for i0 in range(0, SUB, 2):
-                        bank = psum.tile([P, 2, 2, P], F32, tag="bank")
+                        bank = turned.tile([P, 2, 2, P], F32, tag="bank")
                         for u in range(2):
                             for ii in range(2):
                                 first = (2 * g + u) * P
@@ -157,10 +191,24 @@ def tile_geoconv_pb_t_kernel(tc, feat, ag, W_feat, b_feat, g1, be1, W_ag, b_ag, 
                         )
                 load_next_chunk()
 
-            for j in range(CH_TILES):
+            for c in range(FEAT_EARLY):
+                transpose_feat(c)
+
+            for s in range(PE_STAT_TILES):
+                nc.vector.tensor_tensor(out=diagonal[:, s, :], in0=squares[s][:], in1=ident_f32[:], op=ALU.mult)
+            nc.vector.tensor_reduce(out=sum_of_squares[:], in_=diagonal[:], axis=AXIS.X, op=ALU.add)
+            nc.vector.tensor_reduce(out=sum_of_values[:], in_=values[:, :, :, 0], axis=AXIS.X, op=ALU.add)
+            pe_mean = mean_var[:, DVE_STAT_TILES:CH_TILES, 0]
+            pe_var = mean_var[:, DVE_STAT_TILES:CH_TILES, 1]
+            nc.vector.tensor_scalar_mul(out=pe_mean, in0=sum_of_values[:], scalar1=1.0 / POINTS)
+            nc.vector.tensor_mul(out=mean_squared[:], in0=pe_mean, in1=pe_mean)
+            nc.vector.scalar_tensor_tensor(
+                out=pe_var, in0=sum_of_squares[:], scalar=1.0 / POINTS, in1=mean_squared[:], op0=ALU.mult, op1=ALU.subtract
+            )
+            nc.vector.tensor_scalar_max(out=pe_var, in0=pe_var, scalar1=0.0)
+            for j in range(DVE_STAT_TILES):
                 nc.vector.bn_aggr(out=mean_var[:, j, :], in_=stats[:, j, :, :].rearrange("p c s -> p (c s)"))
-            mean = mean_var[:, :, 0]
-            var = mean_var[:, :, 1]
+
             nc.scalar.activation(out=std[:], in_=var, func=ACT.Sqrt, bias=eps[:], scale=1.0)
             for w in range(2):
                 nc.vector.quantize_mx(
@@ -173,9 +221,23 @@ def tile_geoconv_pb_t_kernel(tc, feat, ag, W_feat, b_feat, g1, be1, W_ag, b_ag, 
             nc.vector.tensor_mul(out=scaled_mean[:], in0=mean, in1=bn_scale[:])
             nc.vector.tensor_sub(out=bn_shift[:], in0=shift, in1=scaled_mean[:])
 
-        with tc.tile_pool(name="stage", bufs=2, reuse_waits="tile") as stage, tc.tile_pool(
-            name="codes", bufs=3, reuse_waits="tile"
-        ) as codes_pool:
+            for j in range(CH_TILES):
+                nc.vector.tensor_scalar(
+                    out=ag_t[:, j, :],
+                    in0=ag_t[:, j, :],
+                    scalar1=bn_scale[:, j : j + 1],
+                    scalar2=bn_shift[:, j : j + 1],
+                    op0=ALU.mult,
+                    op1=ALU.add,
+                )
+
+            for c in range(FEAT_EARLY, N_CHUNKS):
+                transpose_feat(c)
+
+        with ExitStack() as part2:
+            stage = part2.enter_context(tc.tile_pool(name="stage", bufs=2, reuse_waits="tile"))
+            codes_pool = part2.enter_context(tc.tile_pool(name="codes", bufs=3, reuse_waits="tile"))
+            psum = part2.enter_context(tc.psum_pool(name="psum", bufs=PSUM_BANKS, reuse_waits="tile"))
             h_grouped = {}
             operands = {}
             products = {}
@@ -191,8 +253,8 @@ def tile_geoconv_pb_t_kernel(tc, feat, ag, W_feat, b_feat, g1, be1, W_ag, b_ag, 
                     )
 
             def quantise_feat(c):
-                feat_codes = codes_pool.tile([P, PASSES, CHUNK], U32, align_bytes=64)
-                feat_scales = codes_pool.tile([P, PASSES, CHUNK], U8, align_bytes=64)
+                feat_codes = codes_pool.tile([P, PASSES, CHUNK], U32, align_bytes=64, bufs=FEAT_AHEAD + 2)
+                feat_scales = codes_pool.tile([P, PASSES, CHUNK], U8, align_bytes=64, bufs=FEAT_AHEAD + 2)
                 nc.vector.quantize_mx(
                     out=feat_codes[:].rearrange("p g q -> p (g q)").bitcast(FP8X4),
                     scales=feat_scales[:].rearrange("p g q -> p (g q)"),
@@ -234,20 +296,13 @@ def tile_geoconv_pb_t_kernel(tc, feat, ag, W_feat, b_feat, g1, be1, W_ag, b_ag, 
                     if i % 2 == 1:
                         nc.sync.dma_start(out=out_chunks[c][:, i - 1 : i + 1, :], in_=result[:, i - 1 : i + 1, :])
 
-            for j in range(CH_TILES):
-                nc.vector.tensor_scalar(
-                    out=ag_t[:, j, :],
-                    in0=ag_t[:, j, :],
-                    scalar1=bn_scale[:, j : j + 1],
-                    scalar2=bn_shift[:, j : j + 1],
-                    op0=ALU.mult,
-                    op1=ALU.add,
-                )
-
+            for c in range(FEAT_AHEAD - 1):
+                quantise_feat(c)
             for k in range(-1, N_CHUNKS + 1):
                 if k + 1 < N_CHUNKS:
                     relu_and_regroup(k + 1)
-                    quantise_feat(k + 1)
+                if k + FEAT_AHEAD < N_CHUNKS:
+                    quantise_feat(k + FEAT_AHEAD)
                 if 0 <= k < N_CHUNKS:
                     quantise_h(k)
                     multiply(k)

@@ -33,6 +33,7 @@ PE_STAT_TILES = 3
 DVE_STAT_TILES = CH_TILES - PE_STAT_TILES
 FEAT_EARLY = 2
 FEAT_AHEAD = 3
+VECTOR_REGROUPS_EVERY = 4
 RUN = 4
 
 FLOPS = 2 * POINTS * (CHANNELS + CHANNELS) * COUT
@@ -246,11 +247,12 @@ def tile_geoconv_pb_t_kernel(tc, feat, ag, W_feat, b_feat, g1, be1, W_ag, b_ag, 
                 columns = slice(c * CHUNK, (c + 1) * CHUNK)
                 h_grouped[c] = stage.tile([P, PASSES, CHUNK, PACK], BF16, align_bytes=64, name="h_grouped")
                 for g in range(PASSES):
-                    nc.scalar.activation(
-                        out=by_runs_dst(h_grouped[c][:, g, :, :]),
-                        in_=by_runs_src(ag_t[:, g * PACK : (g + 1) * PACK, columns]),
-                        func=ACT.Relu,
-                    )
+                    grouped = by_runs_dst(h_grouped[c][:, g, :, :])
+                    rows = by_runs_src(ag_t[:, g * PACK : (g + 1) * PACK, columns])
+                    if g == PASSES - 1 and c % VECTOR_REGROUPS_EVERY == VECTOR_REGROUPS_EVERY - 1:
+                        nc.vector.tensor_scalar_max(out=grouped, in0=rows, scalar1=0.0)
+                    else:
+                        nc.scalar.activation(out=grouped, in_=rows, func=ACT.Relu)
 
             def quantise_feat(c):
                 feat_codes = codes_pool.tile([P, PASSES, CHUNK], U32, align_bytes=64, bufs=FEAT_AHEAD + 2)
@@ -265,11 +267,12 @@ def tile_geoconv_pb_t_kernel(tc, feat, ag, W_feat, b_feat, g1, be1, W_ag, b_ag, 
             def quantise_h(c):
                 h_codes = codes_pool.tile([P, PASSES, CHUNK], U32, align_bytes=64)
                 h_scales = codes_pool.tile([P, PASSES, CHUNK], U8, align_bytes=64)
-                nc.vector.quantize_mx(
-                    out=h_codes[:].rearrange("p g q -> p (g q)").bitcast(FP8X4),
-                    scales=h_scales[:].rearrange("p g q -> p (g q)"),
-                    in_=h_grouped[c][:].rearrange("p g q t -> p (g q t)"),
-                )
+                for g in range(PASSES):
+                    nc.vector.quantize_mx(
+                        out=h_codes[:, g, :].bitcast(FP8X4),
+                        scales=h_scales[:, g, :],
+                        in_=h_grouped[c][:, g, :, :].rearrange("p q t -> p (q t)"),
+                    )
                 operands[c].append((h_codes, h_scales))
 
             def multiply(c):
@@ -293,8 +296,7 @@ def tile_geoconv_pb_t_kernel(tc, feat, ag, W_feat, b_feat, g1, be1, W_ag, b_ag, 
                 result = stage.tile([P, SUB, COUT], F32)
                 for i in range(SUB):
                     nc.vector.tensor_tensor(out=result[:, i, :], in0=products[c][i][:], in1=bias[:], op=ALU.add)
-                    if i % 2 == 1:
-                        nc.sync.dma_start(out=out_chunks[c][:, i - 1 : i + 1, :], in_=result[:, i - 1 : i + 1, :])
+                    nc.sync.dma_start(out=out_chunks[c][:, i, :], in_=result[:, i, :])
 
             for c in range(FEAT_AHEAD - 1):
                 quantise_feat(c)

@@ -32,7 +32,7 @@ NATURAL_BUFS = 5
 PE_STAT_TILES = 3
 DVE_STAT_TILES = CH_TILES - PE_STAT_TILES
 FEAT_EARLY = 2
-FEAT_AHEAD = 3
+FEAT_AHEAD = 5
 VECTOR_REGROUPS_EVERY = 4
 RUN = 4
 

from contextlib import ExitStack

import concourse.mybir as mybir
from concourse.masks import make_identity

BF16 = mybir.dt.bfloat16
F32 = mybir.dt.float32
U32 = mybir.dt.uint32
U8 = mybir.dt.uint8
FP8X4 = mybir.dt.float8_e4m3fn_x4
ALU = mybir.AluOpType
ACT = mybir.ActivationFunctionType
AXIS = mybir.AxisListType

P = 128
PACK = 4
K_PASS = P * PACK

POINTS = 8 * 512
CHANNELS = 1024
COUT = 512
BN_EPS = 1e-5

SUB = 4
CHUNK = P * SUB
N_CHUNKS = POINTS // CHUNK
PASSES = CHANNELS // K_PASS
CH_TILES = CHANNELS // P
BN_STATS_DIM = 6
PSUM_BANKS = 8
NATURAL_BUFS = 5
PE_STAT_TILES = 3
DVE_STAT_TILES = CH_TILES - PE_STAT_TILES
FEAT_EARLY = 2
FEAT_AHEAD = 5
VECTOR_REGROUPS_EVERY = 4
RUN = 4

FLOPS = 2 * POINTS * (CHANNELS + CHANNELS) * COUT


def by_runs_src(rows):
    return rows.rearrange("p t (c i) -> p c t i", i=RUN)


def by_runs_dst(grouped):
    return grouped.rearrange("p (c i) t -> p c t i", i=RUN)


def tile_geoconv_pb_t_kernel(tc, feat, ag, W_feat, b_feat, g1, be1, W_ag, b_ag, out):
    nc = tc.nc
    feat_chunks = feat.flatten_outer_dims().rearrange("(c p i) k -> c p i k", p=P, i=SUB)
    ag_chunks = ag.flatten_outer_dims().rearrange("(c p i) k -> c p i k", p=P, i=SUB)
    out_chunks = out.flatten_outer_dims().rearrange("(c p i) n -> c p i n", p=P, i=SUB)

    with ExitStack() as ctx:
        ctx.enter_context(tc.manual_schedule())
        keep = ctx.enter_context(tc.tile_pool(name="keep", bufs=1))

        ident_bf16 = keep.tile([P, P], BF16)
        make_identity(nc, ident_bf16[:])
        ident_f32 = keep.tile([P, P], F32)
        make_identity(nc, ident_f32[:])

        eps = keep.tile([P, 1], F32)
        nc.vector.memset(eps[:], BN_EPS)
        table_warmer = keep.tile([P, 1], F32)
        nc.scalar.activation(out=table_warmer[:], in_=eps[:], func=ACT.Sqrt)

        ones = keep.tile([P, P], BF16)
        nc.vector.memset(ones[:], 1.0)
        vector_rows = keep.tile([P, P], BF16)
        nc.vector.memset(vector_rows[:], 0.0)
        nc.scalar.dma_start(out=vector_rows[0:CH_TILES, :], in_=g1.rearrange("(j p) -> j p", p=P))
        nc.scalar.dma_start(out=vector_rows[CH_TILES : 2 * CH_TILES, :], in_=be1.rearrange("(j p) -> j p", p=P))
        bias_rows = keep.tile([P, COUT], BF16)
        nc.vector.memset(bias_rows[:], 0.0)
        nc.scalar.dma_start(out=bias_rows[0:1, :], in_=b_feat.rearrange("(o n) -> o n", o=1))
        nc.scalar.dma_start(out=bias_rows[1:2, :], in_=b_ag.rearrange("(o n) -> o n", o=1))
        gain_shift = keep.tile([P, 2 * CH_TILES], F32)
        gain = gain_shift[:, 0:CH_TILES]
        shift = gain_shift[:, CH_TILES : 2 * CH_TILES]
        bias = keep.tile([P, COUT], F32)

        ag_t = keep.tile([P, CH_TILES, POINTS], BF16)
        feat_grouped = keep.tile([P, N_CHUNKS, PASSES, CHUNK * PACK], BF16, align_bytes=64)
        feat_grouped_words = feat_grouped[:].bitcast(F32)
        w_codes = keep.tile([P, 2, PASSES, COUT], U32, align_bytes=64)
        w_scales = keep.tile([P, 2, PASSES, COUT], U8, align_bytes=64)
        stats = keep.tile([P, DVE_STAT_TILES, N_CHUNKS, BN_STATS_DIM], F32)
        diagonal = keep.tile([P, PE_STAT_TILES, P], F32)
        sum_of_squares = keep.tile([P, PE_STAT_TILES], F32)
        sum_of_values = keep.tile([P, PE_STAT_TILES], F32)
        mean_squared = keep.tile([P, PE_STAT_TILES], F32)
        mean_var = keep.tile([P, CH_TILES, 2], F32)
        mean = mean_var[:, :, 0]
        var = mean_var[:, :, 1]
        std = keep.tile([P, CH_TILES], F32)
        inv_std = keep.tile([P, CH_TILES], F32)
        bn_scale = keep.tile([P, CH_TILES], F32)
        scaled_mean = keep.tile([P, CH_TILES], F32)
        bn_shift = keep.tile([P, CH_TILES], F32)

        with ExitStack() as part1:
            w_stage = part1.enter_context(tc.tile_pool(name="w_stage", bufs=1))
            natural = part1.enter_context(tc.tile_pool(name="natural", bufs=NATURAL_BUFS))
            sums_psum = part1.enter_context(tc.psum_pool(name="sums_psum", bufs=1))
            turned = part1.enter_context(tc.psum_pool(name="turned", bufs=PSUM_BANKS - PE_STAT_TILES - 1))
            squares = [sums_psum.tile([P, P], F32, name="squares%d" % s) for s in range(PE_STAT_TILES)]
            values = sums_psum.tile([P, PE_STAT_TILES, N_CHUNKS * SUB, 2], F32)

            sources = [ag_chunks[c] for c in range(N_CHUNKS)] + [feat_chunks[c] for c in range(N_CHUNKS)]
            loaded = []

            def load_next_chunk():
                if len(loaded) < len(sources):
                    chunk = natural.tile([P, SUB, CHANNELS], BF16, tag="natural", name="chunk")
                    nc.sync.dma_start(out=chunk[:], in_=sources[len(loaded)])
                    loaded.append(chunk)

            for k in range(NATURAL_BUFS):
                load_next_chunk()

            wf_raw = w_stage.tile([P, PASSES * 2, 2 * COUT], BF16)
            nc.sync.dma_start(out=wf_raw[:], in_=W_feat.rearrange("(a p e) n -> p a (e n)", p=P, e=2))
            wa_raw = w_stage.tile([P, PASSES * PACK, COUT], BF16)
            nc.sync.dma_start(out=wa_raw[:], in_=W_ag.rearrange("(a p) n -> p a n", p=P))
            w_rows = [wf_raw[:].rearrange("p a (e n) -> p (a e) n", e=2), wa_raw[:]]
            w_grouped = w_stage.tile([P, 2, PASSES, COUT, PACK], BF16, align_bytes=64)
            for w in range(2):
                for g in range(PASSES):
                    nc.gpsimd.tensor_scalar(
                        out=by_runs_dst(w_grouped[:, w, g, :, :]),
                        in0=by_runs_src(w_rows[w][:, g * PACK : (g + 1) * PACK, :]),
                        scalar1=1.0,
                        scalar2=0.0,
                        op0=ALU.mult,
                        op1=ALU.add,
                    )

            for c in range(N_CHUNKS):
                ag_nat = loaded[c]
                columns = slice(c * CHUNK, (c + 1) * CHUNK)
                for j in range(CH_TILES):
                    blocks = [ag_nat[:, i, j * P : (j + 1) * P] for i in range(SUB)]
                    bank = turned.tile([P, SUB, P], BF16, tag="bank")
                    for i in range(SUB):
                        nc.tensor.transpose(bank[:, i, :], blocks[i], ident_bf16[:])
                    nc.scalar.copy(
                        out=ag_t[:, j, columns].bitcast(F32), in_=bank[:].rearrange("p i q -> p (i q)").bitcast(F32)
                    )
                    if j < DVE_STAT_TILES:
                        nc.vector.bn_stats(out=stats[:, j, c, :], in_=ag_t[:, j, columns])
                    else:
                        s = j - DVE_STAT_TILES
                        for i in range(SUB):
                            nc.tensor.matmul(
                                out=squares[s][:],
                                lhsT=blocks[i],
                                rhs=blocks[i],
                                start=(c == 0 and i == 0),
                                stop=(c == N_CHUNKS - 1 and i == SUB - 1),
                            )
                            nc.tensor.matmul(
                                out=values[:, s, c * SUB + i, :], lhsT=blocks[i], rhs=ones[:, 0:2], start=True, stop=True
                            )
                load_next_chunk()

            vector_cols = turned.tile([P, P], BF16, tag="bank")
            nc.tensor.transpose(vector_cols[:], vector_rows[:], ident_bf16[:])
            nc.scalar.copy(out=gain_shift[:], in_=vector_cols[:, 0 : 2 * CH_TILES])
            bias_sum = turned.tile([P, COUT], F32, tag="bank")
            nc.tensor.matmul(out=bias_sum[:], lhsT=ones[:], rhs=bias_rows[:], start=True, stop=True)
            nc.scalar.copy(out=bias[:], in_=bias_sum[:])

            def transpose_feat(c):
                feat_words = loaded[N_CHUNKS + c][:].bitcast(F32)
                for g in range(PASSES):
                    for i0 in range(0, SUB, 2):
                        bank = turned.tile([P, 2, 2, P], F32, tag="bank")
                        for u in range(2):
                            for ii in range(2):
                                first = (2 * g + u) * P
                                nc.tensor.transpose(
                                    bank[:, u, ii, :], feat_words[:, i0 + ii, first : first + P], ident_f32[:]
                                )
                        nc.scalar.copy(
                            out=feat_grouped_words[:, c, g, i0 * P * 2 : (i0 + 2) * P * 2].rearrange(
                                "p (q u) -> p q u", u=2
                            ),
                            in_=bank[:].rearrange("p u i q -> p (i q) u"),
                        )
                load_next_chunk()

            for c in range(FEAT_EARLY):
                transpose_feat(c)

            for s in range(PE_STAT_TILES):
                nc.vector.tensor_tensor(out=diagonal[:, s, :], in0=squares[s][:], in1=ident_f32[:], op=ALU.mult)
            nc.vector.tensor_reduce(out=sum_of_squares[:], in_=diagonal[:], axis=AXIS.X, op=ALU.add)
            nc.vector.tensor_reduce(out=sum_of_values[:], in_=values[:, :, :, 0], axis=AXIS.X, op=ALU.add)
            pe_mean = mean_var[:, DVE_STAT_TILES:CH_TILES, 0]
            pe_var = mean_var[:, DVE_STAT_TILES:CH_TILES, 1]
            nc.vector.tensor_scalar_mul(out=pe_mean, in0=sum_of_values[:], scalar1=1.0 / POINTS)
            nc.vector.tensor_mul(out=mean_squared[:], in0=pe_mean, in1=pe_mean)
            nc.vector.scalar_tensor_tensor(
                out=pe_var, in0=sum_of_squares[:], scalar=1.0 / POINTS, in1=mean_squared[:], op0=ALU.mult, op1=ALU.subtract
            )
            nc.vector.tensor_scalar_max(out=pe_var, in0=pe_var, scalar1=0.0)
            for j in range(DVE_STAT_TILES):
                nc.vector.bn_aggr(out=mean_var[:, j, :], in_=stats[:, j, :, :].rearrange("p c s -> p (c s)"))

            nc.scalar.activation(out=std[:], in_=var, func=ACT.Sqrt, bias=eps[:], scale=1.0)
            for w in range(2):
                nc.vector.quantize_mx(
                    out=w_codes[:, w, :, :].rearrange("p g n -> p (g n)").bitcast(FP8X4),
                    scales=w_scales[:, w, :, :].rearrange("p g n -> p (g n)"),
                    in_=w_grouped[:, w, :, :, :].rearrange("p g n t -> p (g n t)"),
                )
            nc.vector.reciprocal(out=inv_std[:], in_=std[:])
            nc.vector.tensor_mul(out=bn_scale[:], in0=gain, in1=inv_std[:])
            nc.vector.tensor_mul(out=scaled_mean[:], in0=mean, in1=bn_scale[:])
            nc.vector.tensor_sub(out=bn_shift[:], in0=shift, in1=scaled_mean[:])

            for j in range(CH_TILES):
                nc.vector.tensor_scalar(
                    out=ag_t[:, j, :],
                    in0=ag_t[:, j, :],
                    scalar1=bn_scale[:, j : j + 1],
                    scalar2=bn_shift[:, j : j + 1],
                    op0=ALU.mult,
                    op1=ALU.add,
                )

            for c in range(FEAT_EARLY, N_CHUNKS):
                transpose_feat(c)

        with ExitStack() as part2:
            stage = part2.enter_context(tc.tile_pool(name="stage", bufs=2, reuse_waits="tile"))
            codes_pool = part2.enter_context(tc.tile_pool(name="codes", bufs=3, reuse_waits="tile"))
            psum = part2.enter_context(tc.psum_pool(name="psum", bufs=PSUM_BANKS, reuse_waits="tile"))
            h_grouped = {}
            operands = {}
            products = {}

            def relu_and_regroup(c):
                columns = slice(c * CHUNK, (c + 1) * CHUNK)
                h_grouped[c] = stage.tile([P, PASSES, CHUNK, PACK], BF16, align_bytes=64, name="h_grouped")
                for g in range(PASSES):
                    grouped = by_runs_dst(h_grouped[c][:, g, :, :])
                    rows = by_runs_src(ag_t[:, g * PACK : (g + 1) * PACK, columns])
                    if g == PASSES - 1 and c % VECTOR_REGROUPS_EVERY == VECTOR_REGROUPS_EVERY - 1:
                        nc.vector.tensor_scalar_max(out=grouped, in0=rows, scalar1=0.0)
                    else:
                        nc.scalar.activation(out=grouped, in_=rows, func=ACT.Relu)

            def quantise_feat(c):
                feat_codes = codes_pool.tile([P, PASSES, CHUNK], U32, align_bytes=64, bufs=FEAT_AHEAD + 2)
                feat_scales = codes_pool.tile([P, PASSES, CHUNK], U8, align_bytes=64, bufs=FEAT_AHEAD + 2)
                nc.vector.quantize_mx(
                    out=feat_codes[:].rearrange("p g q -> p (g q)").bitcast(FP8X4),
                    scales=feat_scales[:].rearrange("p g q -> p (g q)"),
                    in_=feat_grouped[:, c, :, :].rearrange("p g x -> p (g x)"),
                )
                operands[c] = [(feat_codes, feat_scales)]

            def quantise_h(c):
                h_codes = codes_pool.tile([P, PASSES, CHUNK], U32, align_bytes=64)
                h_scales = codes_pool.tile([P, PASSES, CHUNK], U8, align_bytes=64)
                for g in range(PASSES):
                    nc.vector.quantize_mx(
                        out=h_codes[:, g, :].bitcast(FP8X4),
                        scales=h_scales[:, g, :],
                        in_=h_grouped[c][:, g, :, :].rearrange("p q t -> p (q t)"),
                    )
                operands[c].append((h_codes, h_scales))

            def multiply(c):
                products[c] = [psum.tile([P, COUT], F32, tag="bank", name="product") for i in range(SUB)]
                for w in range(2):
                    codes, scales = operands[c][w]
                    for g in range(PASSES):
                        for i in range(SUB):
                            points = slice(i * P, (i + 1) * P)
                            nc.tensor.matmul_mx(
                                out=products[c][i][:],
                                lhsT=codes[:, g, points].bitcast(FP8X4),
                                lhsT_scale=scales[:, g, points],
                                rhs=w_codes[:, w, g, :].bitcast(FP8X4),
                                rhs_scale=w_scales[:, w, g, :],
                                start=(w == 0 and g == 0),
                                stop=(w == 1 and g == PASSES - 1),
                            )

            def add_bias_and_store(c):
                result = stage.tile([P, SUB, COUT], F32)
                for i in range(SUB):
                    nc.vector.tensor_tensor(out=result[:, i, :], in0=products[c][i][:], in1=bias[:], op=ALU.add)
                    nc.sync.dma_start(out=out_chunks[c][:, i, :], in_=result[:, i, :])

            for c in range(FEAT_AHEAD - 1):
                quantise_feat(c)
            for k in range(-1, N_CHUNKS + 1):
                if k + 1 < N_CHUNKS:
                    relu_and_regroup(k + 1)
                if k + FEAT_AHEAD < N_CHUNKS:
                    quantise_feat(k + FEAT_AHEAD)
                if 0 <= k < N_CHUNKS:
                    quantise_h(k)
                    multiply(k)
                if 0 <= k - 1:
                    add_bias_and_store(k - 1)
